import numpy as np
import ml_dtypes


def mxq(x, axis, fmt="e4m3"):
    dtype, down = {"e4m3": (ml_dtypes.float8_e4m3fn, 7), "e5m2": (ml_dtypes.float8_e5m2, 14)}[fmt]
    v = np.moveaxis(np.asarray(x, np.float32).astype(ml_dtypes.bfloat16).astype(np.float64), axis, -1)
    blocks = v.reshape(v.shape[:-1] + (-1, 32))
    amax = np.abs(blocks).max(-1, keepdims=True)
    byte = np.maximum(np.where(amax > 0, np.frexp(amax)[1] - 1 + 127, 0) - down, 1)
    scale = np.exp2(byte - 127.0)
    codes = (blocks / scale).astype(np.float32).astype(dtype).astype(np.float64)
    return np.moveaxis((codes * scale).reshape(v.shape), -1, axis)


WIDE = False


def mx_kscale(k):
    if not WIDE:
        return np.ones(k)
    levels = np.array([10, -10, 5, -5, 0])
    a = np.random.permutation(np.resize(levels, k // 512 * 4)).reshape(k // 512, 4)
    idx = np.arange(k)
    return np.exp2(a[idx // 512, idx % 128 // 32])


BF16 = ml_dtypes.bfloat16


def bf(x):
    return np.asarray(x, np.float32).astype(BF16)


def f64(x):
    return np.asarray(x).astype(np.float64)


B, CIN, COUT, H, W, NOFF, PAD = 16, 1024, 1024, 8, 7, 9, 4


def setup_inputs():
    s = mx_kscale(CIN)
    inp = {"x%d" % i: bf(np.random.standard_normal((B, CIN, H, W)) * s[None, :, None, None]) for i in range(NOFF)}
    inp["weights"] = bf(np.random.standard_normal((NOFF, COUT, CIN)) * 0.6 / np.sqrt(CIN) / s)
    inp["bias"] = bf(np.random.standard_normal((NOFF, COUT)) * 0.4)
    return inp


def reference(x0, x1, x2, x3, x4, x5, x6, x7, x8, weights, bias):
    xs = [x0, x1, x2, x3, x4, x5, x6, x7, x8]
    wq = mxq(f64(weights), 2, "e4m3")
    bs = f64(bias)
    out = np.zeros((B, COUT, H, W))
    for i in range(NOFF):
        d = i - PAD
        lo, hi = max(0, -d), W - max(0, d)
        xq = mxq(np.ascontiguousarray(f64(xs[i])[:, :, :, lo:hi]), 1, "e4m3")
        y = (wq[i] @ xq.reshape(B, CIN, H * (hi - lo))).reshape(B, COUT, H, hi - lo)
        y = y + bs[i][None, :, None, None]
        out[:, :, :, lo + d:hi + d] += y
    return out

@@ -1,0 +1,229 @@
+import concourse.mybir as mybir
+from concourse.masks import make_identity
+
+BF16 = mybir.dt.bfloat16
+F32 = mybir.dt.float32
+I32 = mybir.dt.int32
+U32 = mybir.dt.uint32
+U8 = mybir.dt.uint8
+FP8X4 = mybir.dt.float8_e4m3fn_x4
+
+B, CIN, COUT, H, W, NOFF, PAD = 16, 1024, 1024, 8, 7, 9, 4
+
+P = 128
+PACK = 4
+PASSES = CIN // (P * PACK)
+PAIRS = PACK // 2
+O_TILES = COUT // P
+
+HALVES = 2
+B_HALF = B // HALVES
+ROWS = B_HALF * H
+SLOTS = 8
+
+T_PER_LOAD = 4
+T_PER_QUANT = 2
+
+SCALAR_SLOTS = 2
+
+OFFSET_ORDER = sorted(range(NOFF), key=lambda i: abs(i - PAD))
+
+FLOPS = 2 * COUT * CIN * B * H * sum(W - abs(i - PAD) for i in range(NOFF))
+
+
+def power_of_two_pieces(count):
+    pieces = []
+    start = 0
+    size = SLOTS
+    while start < count:
+        if size <= count - start:
+            pieces.append((start, size))
+            start += size
+        else:
+            size //= 2
+    return pieces
+
+
+def tile_scatterhorizontal_t_kernel(
+    tc, x0, x1, x2, x3, x4, x5, x6, x7, x8, weights, bias, out
+):
+    nc = tc.nc
+    xs = [x0, x1, x2, x3, x4, x5, x6, x7, x8]
+
+    w_rows = weights.rearrange("i (m t) k -> i m (t k)", t=O_TILES)
+    out_rows = out.rearrange("b (m t) h w -> m b (t h w)", t=O_TILES)
+
+    used = [W - abs(i - PAD) for i in range(NOFF)]
+    padded = [n + n % 2 for n in used]
+
+    with (
+        tc.tile_pool(name="keep", bufs=1) as keep,
+        tc.tile_pool(name="raw", bufs=6) as raw_pool,
+        tc.tile_pool(name="stage", bufs=4) as stage,
+        tc.tile_pool(name="result", bufs=2) as result,
+        tc.psum_pool(name="psum", bufs=1) as psum,
+    ):
+        identity = keep.tile([P, P], F32)
+        make_identity(nc, identity[:])
+
+        bias_raw = keep.tile([P, NOFF, O_TILES], BF16)
+        nc.scalar.dma_start(out=bias_raw[:], in_=bias.rearrange("i (m t) -> m i t", t=O_TILES))
+        bias_sum = keep.tile([P, O_TILES, W], F32)
+        for c in range(W):
+            first = max(0, c + PAD - (W - 1))
+            last = min(NOFF - 1, c + PAD)
+            nc.vector.tensor_reduce(
+                out=bias_sum[:, :, c],
+                in_=bias_raw[:, first : last + 1, :].rearrange("p i t -> p t i"),
+                axis=mybir.AxisListType.X,
+                op=mybir.AluOpType.add,
+            )
+
+        w_codes = [
+            keep.tile([P, O_TILES, PASSES, P], U32, name="w_codes%d" % i, align_bytes=64)
+            for i in range(NOFF)
+        ]
+        w_scales = [
+            keep.tile([P, O_TILES, PASSES, P], U8, name="w_scales%d" % i, align_bytes=64)
+            for i in range(NOFF)
+        ]
+        x_codes = [
+            keep.tile([P, PASSES, padded[i], ROWS], U32, name="x_codes%d" % i, align_bytes=64)
+            for i in range(NOFF)
+        ]
+        x_scales = [
+            keep.tile([P, PASSES, padded[i], ROWS], U8, name="x_scales%d" % i, align_bytes=64)
+            for i in range(NOFF)
+        ]
+        for i in range(NOFF):
+            if padded[i] > used[i]:
+                nc.vector.memset(x_codes[i][:, :, used[i], :].bitcast(I32), 0)
+                nc.vector.memset(x_scales[i][:, :, used[i], :].bitcast(I32), 0)
+
+        for i in OFFSET_ORDER:
+            for load in range(O_TILES // T_PER_LOAD):
+                w_raw = raw_pool.tile([P, T_PER_LOAD * CIN], BF16, tag="raw")
+                nc.sync.dma_start(
+                    out=w_raw[:],
+                    in_=w_rows[i, :, load * T_PER_LOAD * CIN : (load + 1) * T_PER_LOAD * CIN],
+                )
+                w_words = w_raw[:].bitcast(F32).rearrange(
+                    "m (t g q u) -> m t g u q", t=T_PER_LOAD, g=PASSES, u=PAIRS
+                )
+                for quant in range(T_PER_LOAD // T_PER_QUANT):
+                    w_grouped = stage.tile(
+                        [P, T_PER_QUANT * CIN], BF16, tag="grouped", align_bytes=64
+                    )
+                    w_grouped_words = w_grouped[:].bitcast(F32).rearrange(
+                        "q (t g m u) -> q t g m u", t=T_PER_QUANT, g=PASSES, u=PAIRS
+                    )
+                    first_t = load * T_PER_LOAD + quant * T_PER_QUANT
+                    for n in range(T_PER_QUANT):
+                        t = first_t + n
+                        flipped = psum.tile([P, PASSES, PAIRS, P], F32, tag="bank%d" % t)
+                        for g in range(PASSES):
+                            for u in range(PAIRS):
+                                nc.tensor.transpose(
+                                    flipped[:, g, u, :],
+                                    w_words[:, t % T_PER_LOAD, g, u, :],
+                                    identity[:],
+                                )
+                        copy = nc.vector.tensor_copy if t % 4 == 3 else nc.scalar.copy
+                        copy(
+                            out=w_grouped_words[:, n],
+                            in_=flipped[:].rearrange("q g u m -> q g m u"),
+                        )
+                    nc.vector.quantize_mx(
+                        out=w_codes[i][:, first_t : first_t + T_PER_QUANT]
+                        .rearrange("q t g m -> q (t g m)")
+                        .bitcast(FP8X4),
+                        scales=w_scales[i][:, first_t : first_t + T_PER_QUANT].rearrange(
+                            "q t g m -> q (t g m)"
+                        ),
+                        in_=w_grouped[:],
+                    )
+
+        for half in range(HALVES):
+            batches = slice(half * B_HALF, (half + 1) * B_HALF)
+            sums = [
+                psum.tile([P, SLOTS, ROWS], F32, tag="bank%d" % t, name="sums%d" % t)
+                for t in range(O_TILES)
+            ]
+            for i in OFFSET_ORDER:
+                d = i - PAD
+                first_source = max(0, -d)
+                first_slot = max(0, d)
+
+                x_raw = raw_pool.tile([P, B_HALF, PASSES, PACK * H * W], BF16, tag="raw")
+                nc.sync.dma_start(
+                    out=x_raw[:],
+                    in_=xs[i].rearrange(
+                        "b (g p j) h w -> p b g (j h w)", g=PASSES, p=P, j=PACK
+                    )[:, batches],
+                )
+                x_columns = x_raw[:].rearrange(
+                    "p b g (j h w) -> p g w b h j", j=PACK, h=H, w=W
+                )
+                x_grouped = stage.tile(
+                    [P, PASSES, W, ROWS * PACK], BF16, tag="grouped", align_bytes=64
+                )
+                x_grouped_values = x_grouped[:].rearrange(
+                    "p g s (b h j) -> p g s b h j", b=B_HALF, h=H, j=PACK
+                )
+                vector_slots = used[i] - SCALAR_SLOTS
+                for g in range(PASSES):
+                    nc.vector.tensor_copy(
+                        out=x_grouped_values[:, g, 0:vector_slots],
+                        in_=x_columns[:, g, first_source : first_source + vector_slots],
+                    )
+                    for s in range(vector_slots, used[i]):
+                        nc.scalar.copy(
+                            out=x_grouped_values[:, g, s],
+                            in_=x_columns[:, g, first_source + s],
+                        )
+                for g in range(PASSES):
+                    for s, n in power_of_two_pieces(used[i]):
+                        nc.vector.quantize_mx(
+                            out=x_codes[i][:, g, s : s + n]
+                            .rearrange("p s r -> p (s r)")
+                            .bitcast(FP8X4),
+                            scales=x_scales[i][:, g, s : s + n].rearrange("p s r -> p (s r)"),
+                            in_=x_grouped[:, g, s : s + n].rearrange("p s v -> p (s v)"),
+                        )
+
+                for t in range(O_TILES):
+                    for g in range(PASSES):
+                        for s, n in power_of_two_pieces(padded[i]):
+                            nc.tensor.matmul_mx(
+                                out=sums[t][
+                                    :, first_slot + s : first_slot + s + n
+                                ].rearrange("m s r -> m (s r)"),
+                                lhsT=w_codes[i][:, t, g, :].bitcast(FP8X4),
+                                lhsT_scale=w_scales[i][:, t, g, :],
+                                rhs=x_codes[i][:, g, s : s + n]
+                                .rearrange("p s r -> p (s r)")
+                                .bitcast(FP8X4),
+                                rhs_scale=x_scales[i][:, g, s : s + n].rearrange(
+                                    "p s r -> p (s r)"
+                                ),
+                                start=(i == OFFSET_ORDER[0] and g == 0),
+                                stop=(
+                                    i == OFFSET_ORDER[-1]
+                                    and g == PASSES - 1
+                                    and s + n == padded[i]
+                                ),
+                            )
+
+            finished = result.tile([P, B_HALF, O_TILES, H, W], F32)
+            for t in range(O_TILES):
+                nc.vector.tensor_tensor(
+                    out=finished[:, :, t],
+                    in0=sums[t][:, 0:W, :].rearrange("m c (b h) -> m b h c", b=B_HALF),
+                    in1=bias_sum[:, t, :].unsqueeze(1).unsqueeze(1).to_broadcast([P, B_HALF, H, W]),
+                    op=mybir.AluOpType.add,
+                )
+            store_queue = nc.sync if half == HALVES - 1 else nc.gpsimd
+            store_queue.dma_start(
+                out=out_rows[:, batches],
+                in_=finished[:].rearrange("m b t h w -> m b (t h w)"),
+            )

@@ -24,7 +24,9 @@ SLOTS = 8
 T_PER_LOAD = 4
 T_PER_QUANT = 2
 
-SCALAR_SLOTS = 2
+T_PER_STORE = 4
+
+SCALAR_SHARE = 3
 
 OFFSET_ORDER = sorted(range(NOFF), key=lambda i: abs(i - PAD))
 
@@ -51,7 +53,7 @@ def tile_scatterhorizontal_t_kernel(
     xs = [x0, x1, x2, x3, x4, x5, x6, x7, x8]
 
     w_rows = weights.rearrange("i (m t) k -> i m (t k)", t=O_TILES)
-    out_rows = out.rearrange("b (m t) h w -> m b (t h w)", t=O_TILES)
+    out_rows = out.rearrange("b (m t) h w -> m b t (h w)", t=O_TILES)
 
     used = [W - abs(i - PAD) for i in range(NOFF)]
     padded = [n + n % 2 for n in used]
@@ -60,7 +62,7 @@ def tile_scatterhorizontal_t_kernel(
         tc.tile_pool(name="keep", bufs=1) as keep,
         tc.tile_pool(name="raw", bufs=6) as raw_pool,
         tc.tile_pool(name="stage", bufs=4) as stage,
-        tc.tile_pool(name="result", bufs=2) as result,
+        tc.tile_pool(name="result", bufs=HALVES * O_TILES // T_PER_STORE) as result,
         tc.psum_pool(name="psum", bufs=1) as psum,
     ):
         identity = keep.tile([P, P], F32)
@@ -143,6 +145,7 @@ def tile_scatterhorizontal_t_kernel(
                         in_=w_grouped[:],
                     )
 
+        waiting_stores = []
         for half in range(HALVES):
             batches = slice(half * B_HALF, (half + 1) * B_HALF)
             sums = [
@@ -162,24 +165,24 @@ def tile_scatterhorizontal_t_kernel(
                     )[:, batches],
                 )
                 x_columns = x_raw[:].rearrange(
-                    "p b g (j h w) -> p g w b h j", j=PACK, h=H, w=W
+                    "p b g (j h w) -> p g b w h j", j=PACK, h=H, w=W
                 )
                 x_grouped = stage.tile(
                     [P, PASSES, W, ROWS * PACK], BF16, tag="grouped", align_bytes=64
                 )
                 x_grouped_values = x_grouped[:].rearrange(
-                    "p g s (b h j) -> p g s b h j", b=B_HALF, h=H, j=PACK
+                    "p g s (b h j) -> p g b s h j", b=B_HALF, h=H, j=PACK
                 )
-                vector_slots = used[i] - SCALAR_SLOTS
+                vector_slots = used[i] - used[i] // SCALAR_SHARE
                 for g in range(PASSES):
                     nc.vector.tensor_copy(
-                        out=x_grouped_values[:, g, 0:vector_slots],
-                        in_=x_columns[:, g, first_source : first_source + vector_slots],
+                        out=x_grouped_values[:, g, :, 0:vector_slots],
+                        in_=x_columns[:, g, :, first_source : first_source + vector_slots],
                     )
                     for s in range(vector_slots, used[i]):
                         nc.scalar.copy(
-                            out=x_grouped_values[:, g, s],
-                            in_=x_columns[:, g, first_source + s],
+                            out=x_grouped_values[:, g, :, s],
+                            in_=x_columns[:, g, :, first_source + s],
                         )
                 for g in range(PASSES):
                     for s, n in power_of_two_pieces(used[i]):
@@ -214,16 +217,29 @@ def tile_scatterhorizontal_t_kernel(
                                 ),
                             )
 
-            finished = result.tile([P, B_HALF, O_TILES, H, W], F32)
-            for t in range(O_TILES):
-                nc.vector.tensor_tensor(
-                    out=finished[:, :, t],
-                    in0=sums[t][:, 0:W, :].rearrange("m c (b h) -> m b h c", b=B_HALF),
-                    in1=bias_sum[:, t, :].unsqueeze(1).unsqueeze(1).to_broadcast([P, B_HALF, H, W]),
-                    op=mybir.AluOpType.add,
+            for store in waiting_stores:
+                nc.sync.dma_start(out=store[0], in_=store[1])
+            waiting_stores = []
+
+            for first_t in range(0, O_TILES, T_PER_STORE):
+                finished = result.tile([P, B_HALF, T_PER_STORE, H, W], F32)
+                for n in range(T_PER_STORE):
+                    nc.vector.tensor_tensor(
+                        out=finished[:, :, n],
+                        in0=sums[first_t + n][:, 0:W, :].rearrange(
+                            "m c (b h) -> m b h c", b=B_HALF
+                        ),
+                        in1=bias_sum[:, first_t + n, :]
+                        .unsqueeze(1)
+                        .unsqueeze(1)
+                        .to_broadcast([P, B_HALF, H, W]),
+                        op=mybir.AluOpType.add,
+                    )
+                waiting_stores.append(
+                    (
+                        out_rows[:, batches, first_t : first_t + T_PER_STORE],
+                        finished[:].rearrange("m b t h w -> m b t (h w)"),
+                    )
                 )
-            store_queue = nc.sync if half == HALVES - 1 else nc.gpsimd
-            store_queue.dma_start(
-                out=out_rows[:, batches],
-                in_=finished[:].rearrange("m b t h w -> m b (t h w)"),
-            )
+        for store in waiting_stores:
+            nc.sync.dma_start(out=store[0], in_=store[1])

@@ -21,6 +21,8 @@ B_HALF = B // HALVES
 ROWS = B_HALF * H
 SLOTS = 8
 
+RUN_PITCH = 256
+
 T_PER_LOAD = 4
 T_PER_QUANT = 2
 
@@ -104,7 +106,7 @@ def tile_scatterhorizontal_t_kernel(
 
         for i in OFFSET_ORDER:
             for load in range(O_TILES // T_PER_LOAD):
-                w_raw = raw_pool.tile([P, T_PER_LOAD * CIN], BF16, tag="raw")
+                w_raw = raw_pool.tile([P, T_PER_LOAD * CIN], BF16, tag="raw", align_bytes=256)
                 nc.sync.dma_start(
                     out=w_raw[:],
                     in_=w_rows[i, :, load * T_PER_LOAD * CIN : (load + 1) * T_PER_LOAD * CIN],
@@ -157,14 +159,16 @@ def tile_scatterhorizontal_t_kernel(
                 first_source = max(0, -d)
                 first_slot = max(0, d)
 
-                x_raw = raw_pool.tile([P, B_HALF, PASSES, PACK * H * W], BF16, tag="raw")
+                x_raw = raw_pool.tile(
+                    [P, B_HALF, PASSES, RUN_PITCH], BF16, tag="raw", align_bytes=256
+                )
                 nc.sync.dma_start(
-                    out=x_raw[:],
+                    out=x_raw[:, :, :, 0 : PACK * H * W],
                     in_=xs[i].rearrange(
                         "b (g p j) h w -> p b g (j h w)", g=PASSES, p=P, j=PACK
                     )[:, batches],
                 )
-                x_columns = x_raw[:].rearrange(
+                x_columns = x_raw[:, :, :, 0 : PACK * H * W].rearrange(
                     "p b g (j h w) -> p g b w h j", j=PACK, h=H, w=W
                 )
                 x_grouped = stage.tile(

@@ -21,12 +21,15 @@ B_HALF = B // HALVES
 ROWS = B_HALF * H
 SLOTS = 8
 
+RUN = PACK * H * W
 RUN_PITCH = 256
 
 T_PER_LOAD = 4
 T_PER_QUANT = 2
+FIRST_LOAD_PIECES = 4
 
 T_PER_STORE = 4
+T_PER_LAST_STORE = 4
 
 SCALAR_SHARE = 3
 
@@ -104,146 +107,171 @@ def tile_scatterhorizontal_t_kernel(
                 nc.vector.memset(x_codes[i][:, :, used[i], :].bitcast(I32), 0)
                 nc.vector.memset(x_scales[i][:, :, used[i], :].bitcast(I32), 0)
 
-        for i in OFFSET_ORDER:
-            for load in range(O_TILES // T_PER_LOAD):
-                w_raw = raw_pool.tile([P, T_PER_LOAD * CIN], BF16, tag="raw", align_bytes=256)
+        def load_weights(i, load, pieces):
+            w_raw = raw_pool.tile([P, T_PER_LOAD * CIN], BF16, tag="raw", align_bytes=256)
+            width = T_PER_LOAD * CIN // pieces
+            for piece in range(pieces):
                 nc.sync.dma_start(
-                    out=w_raw[:],
-                    in_=w_rows[i, :, load * T_PER_LOAD * CIN : (load + 1) * T_PER_LOAD * CIN],
+                    out=w_raw[:, piece * width : (piece + 1) * width],
+                    in_=w_rows[
+                        i,
+                        :,
+                        load * T_PER_LOAD * CIN + piece * width : load * T_PER_LOAD * CIN
+                        + (piece + 1) * width,
+                    ],
                 )
-                w_words = w_raw[:].bitcast(F32).rearrange(
-                    "m (t g q u) -> m t g u q", t=T_PER_LOAD, g=PASSES, u=PAIRS
-                )
-                for quant in range(T_PER_LOAD // T_PER_QUANT):
-                    w_grouped = stage.tile(
-                        [P, T_PER_QUANT * CIN], BF16, tag="grouped", align_bytes=64
-                    )
-                    w_grouped_words = w_grouped[:].bitcast(F32).rearrange(
-                        "q (t g m u) -> q t g m u", t=T_PER_QUANT, g=PASSES, u=PAIRS
-                    )
-                    first_t = load * T_PER_LOAD + quant * T_PER_QUANT
-                    for n in range(T_PER_QUANT):
-                        t = first_t + n
-                        flipped = psum.tile([P, PASSES, PAIRS, P], F32, tag="bank%d" % t)
-                        for g in range(PASSES):
-                            for u in range(PAIRS):
-                                nc.tensor.transpose(
-                                    flipped[:, g, u, :],
-                                    w_words[:, t % T_PER_LOAD, g, u, :],
-                                    identity[:],
-                                )
-                        copy = nc.vector.tensor_copy if t % 4 == 3 else nc.scalar.copy
-                        copy(
-                            out=w_grouped_words[:, n],
-                            in_=flipped[:].rearrange("q g u m -> q g m u"),
+            return w_raw
+
+        def flip_weights(w_raw, first_t):
+            w_words = w_raw[:].bitcast(F32).rearrange(
+                "m (t g q u) -> m t g u q", t=T_PER_LOAD, g=PASSES, u=PAIRS
+            )
+            w_grouped = stage.tile([P, T_PER_QUANT * CIN], BF16, tag="grouped", align_bytes=64)
+            w_grouped_words = w_grouped[:].bitcast(F32).rearrange(
+                "q (t g m u) -> q t g m u", t=T_PER_QUANT, g=PASSES, u=PAIRS
+            )
+            for n in range(T_PER_QUANT):
+                t = first_t + n
+                flipped = psum.tile([P, PASSES, PAIRS, P], F32, tag="bank%d" % t)
+                for g in range(PASSES):
+                    for u in range(PAIRS):
+                        nc.tensor.transpose(
+                            flipped[:, g, u, :], w_words[:, t % T_PER_LOAD, g, u, :], identity[:]
                         )
+                copy = nc.vector.tensor_copy if t % 4 == 3 else nc.scalar.copy
+                copy(out=w_grouped_words[:, n], in_=flipped[:].rearrange("q g u m -> q g m u"))
+            return w_grouped
+
+        def quantise_weights(i, first_t, w_grouped):
+            nc.vector.quantize_mx(
+                out=w_codes[i][:, first_t : first_t + T_PER_QUANT]
+                .rearrange("q t g m -> q (t g m)")
+                .bitcast(FP8X4),
+                scales=w_scales[i][:, first_t : first_t + T_PER_QUANT].rearrange(
+                    "q t g m -> q (t g m)"
+                ),
+                in_=w_grouped[:],
+            )
+
+        steps = [(half, i) for half in range(HALVES) for i in OFFSET_ORDER]
+
+        def regroup(half, i):
+            first_source = max(0, PAD - i)
+            x_raw = raw_pool.tile(
+                [P, B_HALF, PASSES, RUN_PITCH], BF16, tag="raw", align_bytes=256
+            )
+            nc.sync.dma_start(
+                out=x_raw[:, :, :, 0:RUN],
+                in_=xs[i].rearrange("b (g p j) h w -> p b g (j h w)", g=PASSES, p=P, j=PACK)[
+                    :, half * B_HALF : (half + 1) * B_HALF
+                ],
+            )
+            x_columns = x_raw[:, :, :, 0:RUN].rearrange(
+                "p b g (j h w) -> p g b w h j", j=PACK, h=H, w=W
+            )
+            x_grouped = stage.tile([P, PASSES, W, ROWS * PACK], BF16, tag="grouped", align_bytes=64)
+            x_grouped_values = x_grouped[:].rearrange(
+                "p g s (b h j) -> p g b s h j", b=B_HALF, h=H, j=PACK
+            )
+            vector_slots = used[i] - used[i] // SCALAR_SHARE
+            for g in range(PASSES):
+                nc.vector.tensor_copy(
+                    out=x_grouped_values[:, g, :, 0:vector_slots],
+                    in_=x_columns[:, g, :, first_source : first_source + vector_slots],
+                )
+                for s in range(vector_slots, used[i]):
+                    nc.scalar.copy(
+                        out=x_grouped_values[:, g, :, s],
+                        in_=x_columns[:, g, :, first_source + s],
+                    )
+            return x_grouped
+
+        def quantise_x(i, x_grouped):
+            for g in range(PASSES):
+                for s, n in power_of_two_pieces(used[i]):
                     nc.vector.quantize_mx(
-                        out=w_codes[i][:, first_t : first_t + T_PER_QUANT]
-                        .rearrange("q t g m -> q (t g m)")
-                        .bitcast(FP8X4),
-                        scales=w_scales[i][:, first_t : first_t + T_PER_QUANT].rearrange(
-                            "q t g m -> q (t g m)"
-                        ),
-                        in_=w_grouped[:],
+                        out=x_codes[i][:, g, s : s + n].rearrange("p s r -> p (s r)").bitcast(FP8X4),
+                        scales=x_scales[i][:, g, s : s + n].rearrange("p s r -> p (s r)"),
+                        in_=x_grouped[:, g, s : s + n].rearrange("p s v -> p (s v)"),
                     )
 
-        waiting_stores = []
-        for half in range(HALVES):
-            batches = slice(half * B_HALF, (half + 1) * B_HALF)
-            sums = [
-                psum.tile([P, SLOTS, ROWS], F32, tag="bank%d" % t, name="sums%d" % t)
-                for t in range(O_TILES)
-            ]
-            for i in OFFSET_ORDER:
-                d = i - PAD
-                first_source = max(0, -d)
-                first_slot = max(0, d)
-
-                x_raw = raw_pool.tile(
-                    [P, B_HALF, PASSES, RUN_PITCH], BF16, tag="raw", align_bytes=256
-                )
-                nc.sync.dma_start(
-                    out=x_raw[:, :, :, 0 : PACK * H * W],
-                    in_=xs[i].rearrange(
-                        "b (g p j) h w -> p b g (j h w)", g=PASSES, p=P, j=PACK
-                    )[:, batches],
-                )
-                x_columns = x_raw[:, :, :, 0 : PACK * H * W].rearrange(
-                    "p b g (j h w) -> p g b w h j", j=PACK, h=H, w=W
-                )
-                x_grouped = stage.tile(
-                    [P, PASSES, W, ROWS * PACK], BF16, tag="grouped", align_bytes=64
-                )
-                x_grouped_values = x_grouped[:].rearrange(
-                    "p g s (b h j) -> p g b s h j", b=B_HALF, h=H, j=PACK
-                )
-                vector_slots = used[i] - used[i] // SCALAR_SHARE
+        def multiply(i, sums):
+            first_slot = max(0, i - PAD)
+            for t in range(O_TILES):
                 for g in range(PASSES):
-                    nc.vector.tensor_copy(
-                        out=x_grouped_values[:, g, :, 0:vector_slots],
-                        in_=x_columns[:, g, :, first_source : first_source + vector_slots],
-                    )
-                    for s in range(vector_slots, used[i]):
-                        nc.scalar.copy(
-                            out=x_grouped_values[:, g, :, s],
-                            in_=x_columns[:, g, :, first_source + s],
-                        )
-                for g in range(PASSES):
-                    for s, n in power_of_two_pieces(used[i]):
-                        nc.vector.quantize_mx(
-                            out=x_codes[i][:, g, s : s + n]
-                            .rearrange("p s r -> p (s r)")
-                            .bitcast(FP8X4),
-                            scales=x_scales[i][:, g, s : s + n].rearrange("p s r -> p (s r)"),
-                            in_=x_grouped[:, g, s : s + n].rearrange("p s v -> p (s v)"),
+                    for s, n in power_of_two_pieces(padded[i]):
+                        nc.tensor.matmul_mx(
+                            out=sums[t][:, first_slot + s : first_slot + s + n].rearrange(
+                                "m s r -> m (s r)"
+                            ),
+                            lhsT=w_codes[i][:, t, g, :].bitcast(FP8X4),
+                            lhsT_scale=w_scales[i][:, t, g, :],
+                            rhs=x_codes[i][:, g, s : s + n].rearrange("p s r -> p (s r)").bitcast(FP8X4),
+                            rhs_scale=x_scales[i][:, g, s : s + n].rearrange("p s r -> p (s r)"),
+                            start=(i == OFFSET_ORDER[0] and g == 0),
+                            stop=(i == OFFSET_ORDER[-1] and g == PASSES - 1 and s + n == padded[i]),
                         )
 
-                for t in range(O_TILES):
-                    for g in range(PASSES):
-                        for s, n in power_of_two_pieces(padded[i]):
-                            nc.tensor.matmul_mx(
-                                out=sums[t][
-                                    :, first_slot + s : first_slot + s + n
-                                ].rearrange("m s r -> m (s r)"),
-                                lhsT=w_codes[i][:, t, g, :].bitcast(FP8X4),
-                                lhsT_scale=w_scales[i][:, t, g, :],
-                                rhs=x_codes[i][:, g, s : s + n]
-                                .rearrange("p s r -> p (s r)")
-                                .bitcast(FP8X4),
-                                rhs_scale=x_scales[i][:, g, s : s + n].rearrange(
-                                    "p s r -> p (s r)"
-                                ),
-                                start=(i == OFFSET_ORDER[0] and g == 0),
-                                stop=(
-                                    i == OFFSET_ORDER[-1]
-                                    and g == PASSES - 1
-                                    and s + n == padded[i]
-                                ),
-                            )
-
-            for store in waiting_stores:
-                nc.sync.dma_start(out=store[0], in_=store[1])
-            waiting_stores = []
-
-            for first_t in range(0, O_TILES, T_PER_STORE):
+        def finish(half, sums, t_per_store):
+            stores = []
+            for first_t in range(0, O_TILES, t_per_store):
                 finished = result.tile([P, B_HALF, T_PER_STORE, H, W], F32)
-                for n in range(T_PER_STORE):
+                for n in range(t_per_store):
                     nc.vector.tensor_tensor(
                         out=finished[:, :, n],
-                        in0=sums[first_t + n][:, 0:W, :].rearrange(
-                            "m c (b h) -> m b h c", b=B_HALF
-                        ),
+                        in0=sums[first_t + n][:, 0:W, :].rearrange("m c (b h) -> m b h c", b=B_HALF),
                         in1=bias_sum[:, first_t + n, :]
                         .unsqueeze(1)
                         .unsqueeze(1)
                         .to_broadcast([P, B_HALF, H, W]),
                         op=mybir.AluOpType.add,
                     )
-                waiting_stores.append(
+                stores.append(
                     (
-                        out_rows[:, batches, first_t : first_t + T_PER_STORE],
-                        finished[:].rearrange("m b t h w -> m b t (h w)"),
+                        out_rows[
+                            :, half * B_HALF : (half + 1) * B_HALF, first_t : first_t + t_per_store
+                        ],
+                        finished[:, :, 0:t_per_store].rearrange("m b t h w -> m b t (h w)"),
                     )
                 )
-        for store in waiting_stores:
+            return stores
+
+        w_pairs = [
+            (i, first_t) for i in OFFSET_ORDER for first_t in range(0, O_TILES, T_PER_QUANT)
+        ]
+        grouped_x = {}
+        flipped_pair = None
+        for n, (i, first_t) in enumerate(w_pairs):
+            if first_t % T_PER_LOAD == 0:
+                w_raw = load_weights(i, first_t // T_PER_LOAD, FIRST_LOAD_PIECES if n == 0 else 1)
+            w_grouped = flip_weights(w_raw, first_t)
+            if flipped_pair is not None:
+                quantise_weights(*flipped_pair)
+            flipped_pair = (i, first_t, w_grouped)
+            if n == len(w_pairs) - 4:
+                grouped_x[0] = regroup(*steps[0])
+            if n == len(w_pairs) - 2:
+                quantise_x(steps[0][1], grouped_x[0])
+        quantise_weights(*flipped_pair)
+        grouped_x[1] = regroup(*steps[1])
+
+        stores = []
+        for n, (half, i) in enumerate(steps):
+            if n + 2 < len(steps):
+                grouped_x[n + 2] = regroup(*steps[n + 2])
+            if n + 2 >= len(steps) - 1:
+                for store in stores:
+                    nc.sync.dma_start(out=store[0], in_=store[1])
+                stores = []
+            if n + 1 < len(steps):
+                quantise_x(steps[n + 1][1], grouped_x[n + 1])
+            if i == OFFSET_ORDER[0]:
+                sums = [
+                    psum.tile([P, SLOTS, ROWS], F32, tag="bank%d" % t, name="sums%d" % t)
+                    for t in range(O_TILES)
+                ]
+            multiply(i, sums)
+            if i == OFFSET_ORDER[-1]:
+                stores = finish(half, sums, T_PER_STORE if half < HALVES - 1 else T_PER_LAST_STORE)
+        for store in stores:
             nc.sync.dma_start(out=store[0], in_=store[1])

@@ -28,6 +28,8 @@ T_PER_LOAD = 4
 T_PER_QUANT = 2
 FIRST_LOAD_PIECES = 4
 
+LEAD = 3
+
 T_PER_STORE = 4
 T_PER_LAST_STORE = 4
 
@@ -236,42 +238,59 @@ def tile_scatterhorizontal_t_kernel(
                 )
             return stores
 
-        w_pairs = [
-            (i, first_t) for i in OFFSET_ORDER for first_t in range(0, O_TILES, T_PER_QUANT)
-        ]
-        grouped_x = {}
-        flipped_pair = None
-        for n, (i, first_t) in enumerate(w_pairs):
-            if first_t % T_PER_LOAD == 0:
-                w_raw = load_weights(i, first_t // T_PER_LOAD, FIRST_LOAD_PIECES if n == 0 else 1)
-            w_grouped = flip_weights(w_raw, first_t)
-            if flipped_pair is not None:
-                quantise_weights(*flipped_pair)
-            flipped_pair = (i, first_t, w_grouped)
-            if n == len(w_pairs) - 4:
-                grouped_x[0] = regroup(*steps[0])
-            if n == len(w_pairs) - 2:
-                quantise_x(steps[0][1], grouped_x[0])
-        quantise_weights(*flipped_pair)
-        grouped_x[1] = regroup(*steps[1])
+        with tc.manual_schedule():
+            w_pairs = [
+                (i, first_t) for i in OFFSET_ORDER for first_t in range(0, O_TILES, T_PER_QUANT)
+            ]
+            last_load = len(w_pairs) - T_PER_LOAD // T_PER_QUANT
+            copied = {}
+            grouped = {}
 
-        stores = []
-        for n, (half, i) in enumerate(steps):
-            if n + 2 < len(steps):
-                grouped_x[n + 2] = regroup(*steps[n + 2])
-            if n + 2 >= len(steps) - 1:
-                for store in stores:
-                    nc.sync.dma_start(out=store[0], in_=store[1])
-                stores = []
-            if n + 1 < len(steps):
-                quantise_x(steps[n + 1][1], grouped_x[n + 1])
-            if i == OFFSET_ORDER[0]:
-                sums = [
-                    psum.tile([P, SLOTS, ROWS], F32, tag="bank%d" % t, name="sums%d" % t)
-                    for t in range(O_TILES)
-                ]
-            multiply(i, sums)
-            if i == OFFSET_ORDER[-1]:
-                stores = finish(half, sums, T_PER_STORE if half < HALVES - 1 else T_PER_LAST_STORE)
-        for store in stores:
-            nc.sync.dma_start(out=store[0], in_=store[1])
+            def weights_pair(n):
+                copied[n] = flip_weights(w_raws[n * T_PER_QUANT // T_PER_LOAD], w_pairs[n][1])
+
+            def weights_codes(n):
+                quantise_weights(w_pairs[n][0], w_pairs[n][1], copied[n])
+
+            w_raws = {}
+            for n in range(last_load):
+                if n * T_PER_QUANT % T_PER_LOAD == 0:
+                    w_raws[n * T_PER_QUANT // T_PER_LOAD] = load_weights(
+                        w_pairs[n][0], w_pairs[n][1] // T_PER_LOAD, FIRST_LOAD_PIECES if n == 0 else 1
+                    )
+                weights_pair(n)
+                if n > 0:
+                    weights_codes(n - 1)
+            grouped[0] = regroup(*steps[0])
+            w_raws[last_load * T_PER_QUANT // T_PER_LOAD] = load_weights(
+                w_pairs[last_load][0], w_pairs[last_load][1] // T_PER_LOAD, 1
+            )
+            weights_pair(last_load)
+            weights_codes(last_load - 1)
+            quantise_x(steps[0][1], grouped[0])
+            weights_pair(last_load + 1)
+            for n in range(1, LEAD):
+                grouped[n] = regroup(*steps[n])
+                if last_load + n - 1 < len(w_pairs):
+                    weights_codes(last_load + n - 1)
+                quantise_x(steps[n][1], grouped[n])
+
+            stores = []
+            for n, (half, i) in enumerate(steps):
+                if n + LEAD < len(steps):
+                    grouped[n + LEAD] = regroup(*steps[n + LEAD])
+                    quantise_x(steps[n + LEAD][1], grouped[n + LEAD])
+                if n + LEAD >= len(steps) - 1:
+                    for store in stores:
+                        nc.sync.dma_start(out=store[0], in_=store[1])
+                    stores = []
+                if i == OFFSET_ORDER[0]:
+                    sums = [
+                        psum.tile([P, SLOTS, ROWS], F32, tag="bank%d" % t, name="sums%d" % t)
+                        for t in range(O_TILES)
+                    ]
+                multiply(i, sums)
+                if i == OFFSET_ORDER[-1]:
+                    stores = finish(half, sums, T_PER_STORE if half < HALVES - 1 else T_PER_LAST_STORE)
+            for store in stores:
+                nc.sync.dma_start(out=store[0], in_=store[1])

@@ -28,7 +28,7 @@ T_PER_LOAD = 4
 T_PER_QUANT = 2
 FIRST_LOAD_PIECES = 4
 
-LEAD = 3
+LEAD = 2
 
 T_PER_STORE = 4
 T_PER_LAST_STORE = 4
@@ -87,6 +87,11 @@ def tile_scatterhorizontal_t_kernel(
                 axis=mybir.AxisListType.X,
                 op=mybir.AluOpType.add,
             )
+
+        bias_rows = keep.tile([P, O_TILES, H, W], F32)
+        nc.vector.tensor_copy(
+            out=bias_rows[:], in_=bias_sum[:].unsqueeze(2).to_broadcast([P, O_TILES, H, W])
+        )
 
         w_codes = [
             keep.tile([P, O_TILES, PASSES, P], U32, name="w_codes%d" % i, align_bytes=64)
@@ -197,22 +202,27 @@ def tile_scatterhorizontal_t_kernel(
                         in_=x_grouped[:, g, s : s + n].rearrange("p s v -> p (s v)"),
                     )
 
-        def multiply(i, sums):
-            first_slot = max(0, i - PAD)
+        def multiply(offsets, sums):
             for t in range(O_TILES):
-                for g in range(PASSES):
-                    for s, n in power_of_two_pieces(padded[i]):
-                        nc.tensor.matmul_mx(
-                            out=sums[t][:, first_slot + s : first_slot + s + n].rearrange(
-                                "m s r -> m (s r)"
-                            ),
-                            lhsT=w_codes[i][:, t, g, :].bitcast(FP8X4),
-                            lhsT_scale=w_scales[i][:, t, g, :],
-                            rhs=x_codes[i][:, g, s : s + n].rearrange("p s r -> p (s r)").bitcast(FP8X4),
-                            rhs_scale=x_scales[i][:, g, s : s + n].rearrange("p s r -> p (s r)"),
-                            start=(i == OFFSET_ORDER[0] and g == 0),
-                            stop=(i == OFFSET_ORDER[-1] and g == PASSES - 1 and s + n == padded[i]),
-                        )
+                for i in offsets:
+                    first_slot = max(0, i - PAD)
+                    for g in range(PASSES):
+                        for s, n in power_of_two_pieces(padded[i]):
+                            nc.tensor.matmul_mx(
+                                out=sums[t][:, first_slot + s : first_slot + s + n].rearrange(
+                                    "m s r -> m (s r)"
+                                ),
+                                lhsT=w_codes[i][:, t, g, :].bitcast(FP8X4),
+                                lhsT_scale=w_scales[i][:, t, g, :],
+                                rhs=x_codes[i][:, g, s : s + n]
+                                .rearrange("p s r -> p (s r)")
+                                .bitcast(FP8X4),
+                                rhs_scale=x_scales[i][:, g, s : s + n].rearrange("p s r -> p (s r)"),
+                                start=(i == OFFSET_ORDER[0] and g == 0),
+                                stop=(
+                                    i == OFFSET_ORDER[-1] and g == PASSES - 1 and s + n == padded[i]
+                                ),
+                            )
 
         def finish(half, sums, t_per_store):
             stores = []
@@ -237,6 +247,37 @@ def tile_scatterhorizontal_t_kernel(
                     )
                 )
             return stores
+
+        def evacuate(sums):
+            emptied = []
+            for first_t in range(0, O_TILES, T_PER_STORE):
+                finished = result.tile([P, B_HALF, T_PER_STORE, H, W], F32)
+                for n in range(T_PER_STORE):
+                    nc.scalar.copy(
+                        out=finished[:, :, n],
+                        in_=sums[first_t + n][:, 0:W, :].rearrange("m c (b h) -> m b h c", b=B_HALF),
+                    )
+                emptied.append(finished)
+            return emptied
+
+        def add_bias_and_store(half, emptied):
+            for piece, finished in enumerate(emptied):
+                first_t = piece * T_PER_STORE
+                nc.vector.tensor_tensor(
+                    out=finished[:].rearrange("m b t h w -> m b (t h w)"),
+                    in0=finished[:].rearrange("m b t h w -> m b (t h w)"),
+                    in1=bias_rows[:, first_t : first_t + T_PER_STORE]
+                    .rearrange("m t h w -> m (t h w)")
+                    .unsqueeze(1)
+                    .to_broadcast([P, B_HALF, T_PER_STORE * H * W]),
+                    op=mybir.AluOpType.add,
+                )
+                nc.sync.dma_start(
+                    out=out_rows[
+                        :, half * B_HALF : (half + 1) * B_HALF, first_t : first_t + T_PER_STORE
+                    ],
+                    in_=finished[:].rearrange("m b t h w -> m b t (h w)"),
+                )
 
         with tc.manual_schedule():
             w_pairs = [
@@ -269,28 +310,30 @@ def tile_scatterhorizontal_t_kernel(
             weights_codes(last_load - 1)
             quantise_x(steps[0][1], grouped[0])
             weights_pair(last_load + 1)
-            for n in range(1, LEAD):
-                grouped[n] = regroup(*steps[n])
-                if last_load + n - 1 < len(w_pairs):
-                    weights_codes(last_load + n - 1)
-                quantise_x(steps[n][1], grouped[n])
+            def make_ready(k):
+                grouped[k] = regroup(*steps[k])
+                if last_load + k - 1 < len(w_pairs):
+                    weights_codes(last_load + k - 1)
+                quantise_x(steps[k][1], grouped[k])
 
-            stores = []
+            for k in range(1, LEAD):
+                make_ready(k)
+
             for n, (half, i) in enumerate(steps):
                 if n + LEAD < len(steps):
-                    grouped[n + LEAD] = regroup(*steps[n + LEAD])
-                    quantise_x(steps[n + LEAD][1], grouped[n + LEAD])
-                if n + LEAD >= len(steps) - 1:
-                    for store in stores:
-                        nc.sync.dma_start(out=store[0], in_=store[1])
-                    stores = []
+                    make_ready(n + LEAD)
+                if n + LEAD == len(steps) - 1:
+                    add_bias_and_store(0, emptied)
                 if i == OFFSET_ORDER[0]:
                     sums = [
                         psum.tile([P, SLOTS, ROWS], F32, tag="bank%d" % t, name="sums%d" % t)
                         for t in range(O_TILES)
                     ]
-                multiply(i, sums)
                 if i == OFFSET_ORDER[-1]:
-                    stores = finish(half, sums, T_PER_STORE if half < HALVES - 1 else T_PER_LAST_STORE)
-            for store in stores:
+                    multiply(OFFSET_ORDER[-2:], sums)
+                    if half < HALVES - 1:
+                        emptied = evacuate(sums)
+                elif i != OFFSET_ORDER[-2]:
+                    multiply([i], sums)
+            for store in finish(HALVES - 1, sums, T_PER_LAST_STORE):
                 nc.sync.dma_start(out=store[0], in_=store[1])

@@ -28,10 +28,11 @@ T_PER_LOAD = 4
 T_PER_QUANT = 2
 FIRST_LOAD_PIECES = 4
 
+WARM_UP = 8
 LEAD = 2
 
 T_PER_STORE = 4
-T_PER_LAST_STORE = 4
+LAST_STORES = [4, 4]
 
 SCALAR_SHARE = 3
 
@@ -92,6 +93,9 @@ def tile_scatterhorizontal_t_kernel(
         nc.vector.tensor_copy(
             out=bias_rows[:], in_=bias_sum[:].unsqueeze(2).to_broadcast([P, O_TILES, H, W])
         )
+
+        zeros = keep.tile([P, SLOTS * ROWS], BF16)
+        nc.vector.memset(zeros[:], 0.0)
 
         w_codes = [
             keep.tile([P, O_TILES, PASSES, P], U32, name="w_codes%d" % i, align_bytes=64)
@@ -161,27 +165,30 @@ def tile_scatterhorizontal_t_kernel(
             )
 
         steps = [(half, i) for half in range(HALVES) for i in OFFSET_ORDER]
+        both_passes = list(range(PASSES))
 
-        def regroup(half, i):
-            first_source = max(0, PAD - i)
-            x_raw = raw_pool.tile(
-                [P, B_HALF, PASSES, RUN_PITCH], BF16, tag="raw", align_bytes=256
-            )
+        def step_tiles():
+            x_raw = raw_pool.tile([P, B_HALF, PASSES, RUN_PITCH], BF16, tag="raw", align_bytes=256)
+            x_grouped = stage.tile([P, PASSES, W, ROWS * PACK], BF16, tag="grouped", align_bytes=64)
+            return x_raw, x_grouped
+
+        def load_x(half, i, x_raw, passes):
+            some = slice(passes[0], passes[-1] + 1)
             nc.sync.dma_start(
-                out=x_raw[:, :, :, 0:RUN],
-                in_=xs[i].rearrange("b (g p j) h w -> p b g (j h w)", g=PASSES, p=P, j=PACK)[
-                    :, half * B_HALF : (half + 1) * B_HALF
-                ],
+                out=x_raw[:, :, some, 0:RUN],
+                in_=xs[i].rearrange("b (g p j) h w -> p b g (j h w)", g=PASSES, p=P, j=PACK)[:, half * B_HALF : (half + 1) * B_HALF, some],
             )
+
+        def regroup(i, x_raw, x_grouped, passes):
+            first_source = max(0, PAD - i)
             x_columns = x_raw[:, :, :, 0:RUN].rearrange(
                 "p b g (j h w) -> p g b w h j", j=PACK, h=H, w=W
             )
-            x_grouped = stage.tile([P, PASSES, W, ROWS * PACK], BF16, tag="grouped", align_bytes=64)
             x_grouped_values = x_grouped[:].rearrange(
                 "p g s (b h j) -> p g b s h j", b=B_HALF, h=H, j=PACK
             )
             vector_slots = used[i] - used[i] // SCALAR_SHARE
-            for g in range(PASSES):
+            for g in passes:
                 nc.vector.tensor_copy(
                     out=x_grouped_values[:, g, :, 0:vector_slots],
                     in_=x_columns[:, g, :, first_source : first_source + vector_slots],
@@ -191,10 +198,9 @@ def tile_scatterhorizontal_t_kernel(
                         out=x_grouped_values[:, g, :, s],
                         in_=x_columns[:, g, :, first_source + s],
                     )
-            return x_grouped
 
-        def quantise_x(i, x_grouped):
-            for g in range(PASSES):
+        def quantise_x(i, x_grouped, passes):
+            for g in passes:
                 for s, n in power_of_two_pieces(used[i]):
                     nc.vector.quantize_mx(
                         out=x_codes[i][:, g, s : s + n].rearrange("p s r -> p (s r)").bitcast(FP8X4),
@@ -202,51 +208,18 @@ def tile_scatterhorizontal_t_kernel(
                         in_=x_grouped[:, g, s : s + n].rearrange("p s v -> p (s v)"),
                     )
 
-        def multiply(offsets, sums):
-            for t in range(O_TILES):
-                for i in offsets:
-                    first_slot = max(0, i - PAD)
-                    for g in range(PASSES):
-                        for s, n in power_of_two_pieces(padded[i]):
-                            nc.tensor.matmul_mx(
-                                out=sums[t][:, first_slot + s : first_slot + s + n].rearrange(
-                                    "m s r -> m (s r)"
-                                ),
-                                lhsT=w_codes[i][:, t, g, :].bitcast(FP8X4),
-                                lhsT_scale=w_scales[i][:, t, g, :],
-                                rhs=x_codes[i][:, g, s : s + n]
-                                .rearrange("p s r -> p (s r)")
-                                .bitcast(FP8X4),
-                                rhs_scale=x_scales[i][:, g, s : s + n].rearrange("p s r -> p (s r)"),
-                                start=(i == OFFSET_ORDER[0] and g == 0),
-                                stop=(
-                                    i == OFFSET_ORDER[-1] and g == PASSES - 1 and s + n == padded[i]
-                                ),
-                            )
-
-        def finish(half, sums, t_per_store):
-            stores = []
-            for first_t in range(0, O_TILES, t_per_store):
-                finished = result.tile([P, B_HALF, T_PER_STORE, H, W], F32)
-                for n in range(t_per_store):
-                    nc.vector.tensor_tensor(
-                        out=finished[:, :, n],
-                        in0=sums[first_t + n][:, 0:W, :].rearrange("m c (b h) -> m b h c", b=B_HALF),
-                        in1=bias_sum[:, first_t + n, :]
-                        .unsqueeze(1)
-                        .unsqueeze(1)
-                        .to_broadcast([P, B_HALF, H, W]),
-                        op=mybir.AluOpType.add,
-                    )
-                stores.append(
-                    (
-                        out_rows[
-                            :, half * B_HALF : (half + 1) * B_HALF, first_t : first_t + t_per_store
-                        ],
-                        finished[:, :, 0:t_per_store].rearrange("m b t h w -> m b t (h w)"),
-                    )
+        def products(i, t, g, sums):
+            first_slot = max(0, i - PAD)
+            for s, n in power_of_two_pieces(padded[i]):
+                nc.tensor.matmul_mx(
+                    out=sums[t][:, first_slot + s : first_slot + s + n].rearrange("m s r -> m (s r)"),
+                    lhsT=w_codes[i][:, t, g, :].bitcast(FP8X4),
+                    lhsT_scale=w_scales[i][:, t, g, :],
+                    rhs=x_codes[i][:, g, s : s + n].rearrange("p s r -> p (s r)").bitcast(FP8X4),
+                    rhs_scale=x_scales[i][:, g, s : s + n].rearrange("p s r -> p (s r)"),
+                    start=(i == OFFSET_ORDER[0] and g == 0),
+                    stop=(i == OFFSET_ORDER[-1] and g == PASSES - 1 and s + n == padded[i]),
                 )
-            return stores
 
         def evacuate(sums):
             emptied = []
@@ -260,61 +233,89 @@ def tile_scatterhorizontal_t_kernel(
                 emptied.append(finished)
             return emptied
 
-        def add_bias_and_store(half, emptied):
+        def add_bias(emptied):
             for piece, finished in enumerate(emptied):
-                first_t = piece * T_PER_STORE
                 nc.vector.tensor_tensor(
                     out=finished[:].rearrange("m b t h w -> m b (t h w)"),
                     in0=finished[:].rearrange("m b t h w -> m b (t h w)"),
-                    in1=bias_rows[:, first_t : first_t + T_PER_STORE]
+                    in1=bias_rows[:, piece * T_PER_STORE : (piece + 1) * T_PER_STORE]
                     .rearrange("m t h w -> m (t h w)")
                     .unsqueeze(1)
                     .to_broadcast([P, B_HALF, T_PER_STORE * H * W]),
                     op=mybir.AluOpType.add,
                 )
-                nc.sync.dma_start(
-                    out=out_rows[
-                        :, half * B_HALF : (half + 1) * B_HALF, first_t : first_t + T_PER_STORE
-                    ],
-                    in_=finished[:].rearrange("m b t h w -> m b t (h w)"),
-                )
+
+        def store(half, first_t, count, finished):
+            nc.sync.dma_start(
+                out=out_rows[:, half * B_HALF : (half + 1) * B_HALF, first_t : first_t + count],
+                in_=finished[:, :, 0:count].rearrange("m b t h w -> m b t (h w)"),
+            )
+
+        def finish(half, sums):
+            first_t = 0
+            for count in LAST_STORES:
+                finished = result.tile([P, B_HALF, T_PER_STORE, H, W], F32)
+                for n in range(count):
+                    nc.vector.tensor_tensor(
+                        out=finished[:, :, n],
+                        in0=sums[first_t + n][:, 0:W, :].rearrange("m c (b h) -> m b h c", b=B_HALF),
+                        in1=bias_sum[:, first_t + n, :]
+                        .unsqueeze(1)
+                        .unsqueeze(1)
+                        .to_broadcast([P, B_HALF, H, W]),
+                        op=mybir.AluOpType.add,
+                    )
+                store(half, first_t, count, finished)
+                first_t += count
 
         with tc.manual_schedule():
             w_pairs = [
                 (i, first_t) for i in OFFSET_ORDER for first_t in range(0, O_TILES, T_PER_QUANT)
             ]
-            last_load = len(w_pairs) - T_PER_LOAD // T_PER_QUANT
+            pairs_per_load = T_PER_LOAD // T_PER_QUANT
+            last_load = len(w_pairs) - pairs_per_load
+            w_raws = {}
             copied = {}
-            grouped = {}
+
+            def weights_load(n):
+                w_raws[n // pairs_per_load] = load_weights(
+                    w_pairs[n][0], w_pairs[n][1] // T_PER_LOAD, FIRST_LOAD_PIECES if n == 0 else 1
+                )
 
             def weights_pair(n):
-                copied[n] = flip_weights(w_raws[n * T_PER_QUANT // T_PER_LOAD], w_pairs[n][1])
+                copied[n] = flip_weights(w_raws[n // pairs_per_load], w_pairs[n][1])
 
             def weights_codes(n):
                 quantise_weights(w_pairs[n][0], w_pairs[n][1], copied[n])
 
-            w_raws = {}
             for n in range(last_load):
-                if n * T_PER_QUANT % T_PER_LOAD == 0:
-                    w_raws[n * T_PER_QUANT // T_PER_LOAD] = load_weights(
-                        w_pairs[n][0], w_pairs[n][1] // T_PER_LOAD, FIRST_LOAD_PIECES if n == 0 else 1
-                    )
+                if n % pairs_per_load == 0:
+                    weights_load(n)
                 weights_pair(n)
                 if n > 0:
                     weights_codes(n - 1)
-            grouped[0] = regroup(*steps[0])
-            w_raws[last_load * T_PER_QUANT // T_PER_LOAD] = load_weights(
-                w_pairs[last_load][0], w_pairs[last_load][1] // T_PER_LOAD, 1
-            )
+
+            half, i = steps[0]
+            x_raw, x_grouped = step_tiles()
+            load_x(half, i, x_raw, both_passes)
+            weights_load(last_load)
+            regroup(i, x_raw, x_grouped, both_passes)
+            for n in range(WARM_UP):
+                unread = psum.tile([P, SLOTS * ROWS], F32, tag="bank%d" % (n % T_PER_LOAD))
+                nc.tensor.matmul(unread[:], lhsT=zeros[:, 0:P], rhs=zeros[:], start=True, stop=True)
             weights_pair(last_load)
             weights_codes(last_load - 1)
-            quantise_x(steps[0][1], grouped[0])
+            quantise_x(i, x_grouped, both_passes)
             weights_pair(last_load + 1)
+
             def make_ready(k):
-                grouped[k] = regroup(*steps[k])
+                half, i = steps[k]
+                x_raw, x_grouped = step_tiles()
+                load_x(half, i, x_raw, both_passes)
+                regroup(i, x_raw, x_grouped, both_passes)
                 if last_load + k - 1 < len(w_pairs):
                     weights_codes(last_load + k - 1)
-                quantise_x(steps[k][1], grouped[k])
+                quantise_x(i, x_grouped, both_passes)
 
             for k in range(1, LEAD):
                 make_ready(k)
@@ -323,17 +324,26 @@ def tile_scatterhorizontal_t_kernel(
                 if n + LEAD < len(steps):
                     make_ready(n + LEAD)
                 if n + LEAD == len(steps) - 1:
-                    add_bias_and_store(0, emptied)
+                    add_bias(emptied)
+                    for piece, finished in enumerate(emptied):
+                        store(0, piece * T_PER_STORE, T_PER_STORE, finished)
                 if i == OFFSET_ORDER[0]:
                     sums = [
                         psum.tile([P, SLOTS, ROWS], F32, tag="bank%d" % t, name="sums%d" % t)
                         for t in range(O_TILES)
                     ]
-                if i == OFFSET_ORDER[-1]:
-                    multiply(OFFSET_ORDER[-2:], sums)
+                    for t in range(O_TILES):
+                        for g in both_passes:
+                            products(i, t, g, sums)
+                elif i == OFFSET_ORDER[-1]:
+                    for t in range(O_TILES):
+                        for late in OFFSET_ORDER[-2:]:
+                            for g in both_passes:
+                                products(late, t, g, sums)
                     if half < HALVES - 1:
                         emptied = evacuate(sums)
                 elif i != OFFSET_ORDER[-2]:
-                    multiply([i], sums)
-            for store in finish(HALVES - 1, sums, T_PER_LAST_STORE):
-                nc.sync.dma_start(out=store[0], in_=store[1])
+                    for t in range(O_TILES):
+                        for g in both_passes:
+                            products(i, t, g, sums)
+            finish(HALVES - 1, sums)

@@ -34,8 +34,6 @@ LEAD = 2
 T_PER_STORE = 4
 LAST_STORES = [4, 4]
 
-SCALAR_SHARE = 3
-
 OFFSET_ORDER = sorted(range(NOFF), key=lambda i: abs(i - PAD))
 
 FLOPS = 2 * COUT * CIN * B * H * sum(W - abs(i - PAD) for i in range(NOFF))
@@ -182,21 +180,22 @@ def tile_scatterhorizontal_t_kernel(
         def regroup(i, x_raw, x_grouped, passes):
             first_source = max(0, PAD - i)
             x_columns = x_raw[:, :, :, 0:RUN].rearrange(
-                "p b g (j h w) -> p g b w h j", j=PACK, h=H, w=W
+                "p b g (j h w) -> p g b h j w", j=PACK, h=H, w=W
             )
             x_grouped_values = x_grouped[:].rearrange(
-                "p g s (b h j) -> p g b s h j", b=B_HALF, h=H, j=PACK
+                "p g s (b h j) -> p g b h j s", b=B_HALF, h=H, j=PACK
             )
-            vector_slots = used[i] - used[i] // SCALAR_SHARE
+            scalar_slots = used[i] // 2 if used[i] > 3 else 0
+            vector_slots = used[i] - scalar_slots
             for g in passes:
                 nc.vector.tensor_copy(
-                    out=x_grouped_values[:, g, :, 0:vector_slots],
-                    in_=x_columns[:, g, :, first_source : first_source + vector_slots],
+                    out=x_grouped_values[:, g, :, :, :, 0:vector_slots],
+                    in_=x_columns[:, g, :, :, :, first_source : first_source + vector_slots],
                 )
-                for s in range(vector_slots, used[i]):
+                if scalar_slots > 0:
                     nc.scalar.copy(
-                        out=x_grouped_values[:, g, :, s],
-                        in_=x_columns[:, g, :, first_source + s],
+                        out=x_grouped_values[:, g, :, :, :, vector_slots : used[i]],
+                        in_=x_columns[:, g, :, :, :, first_source + vector_slots : first_source + used[i]],
                     )
 
         def quantise_x(i, x_grouped, passes):

@@ -31,8 +31,13 @@ FIRST_LOAD_PIECES = 4
 WARM_UP = 8
 LEAD = 2
 
+T_PER_ADD = 2
 T_PER_STORE = 4
 LAST_STORES = [4, 4]
+
+MOST_SLOTS = 4
+
+HANDOVER = NOFF - 1 + LEAD
 
 OFFSET_ORDER = sorted(range(NOFF), key=lambda i: abs(i - PAD))
 
@@ -164,6 +169,7 @@ def tile_scatterhorizontal_t_kernel(
 
         steps = [(half, i) for half in range(HALVES) for i in OFFSET_ORDER]
         both_passes = list(range(PASSES))
+        scalar_share = [n // 2 if n > 3 else 0 for n in used]
 
         def step_tiles():
             x_raw = raw_pool.tile([P, B_HALF, PASSES, RUN_PITCH], BF16, tag="raw", align_bytes=256)
@@ -177,7 +183,7 @@ def tile_scatterhorizontal_t_kernel(
                 in_=xs[i].rearrange("b (g p j) h w -> p b g (j h w)", g=PASSES, p=P, j=PACK)[:, half * B_HALF : (half + 1) * B_HALF, some],
             )
 
-        def regroup(i, x_raw, x_grouped, passes):
+        def regroup(i, x_raw, x_grouped, passes, scalar_slots):
             first_source = max(0, PAD - i)
             x_columns = x_raw[:, :, :, 0:RUN].rearrange(
                 "p b g (j h w) -> p g b h j w", j=PACK, h=H, w=W
@@ -185,13 +191,14 @@ def tile_scatterhorizontal_t_kernel(
             x_grouped_values = x_grouped[:].rearrange(
                 "p g s (b h j) -> p g b h j s", b=B_HALF, h=H, j=PACK
             )
-            scalar_slots = used[i] // 2 if used[i] > 3 else 0
             vector_slots = used[i] - scalar_slots
             for g in passes:
-                nc.vector.tensor_copy(
-                    out=x_grouped_values[:, g, :, :, :, 0:vector_slots],
-                    in_=x_columns[:, g, :, :, :, first_source : first_source + vector_slots],
-                )
+                for s in range(0, vector_slots, MOST_SLOTS):
+                    end = min(s + MOST_SLOTS, vector_slots)
+                    nc.vector.tensor_copy(
+                        out=x_grouped_values[:, g, :, :, :, s:end],
+                        in_=x_columns[:, g, :, :, :, first_source + s : first_source + end],
+                    )
                 if scalar_slots > 0:
                     nc.scalar.copy(
                         out=x_grouped_values[:, g, :, :, :, vector_slots : used[i]],
@@ -232,17 +239,20 @@ def tile_scatterhorizontal_t_kernel(
                 emptied.append(finished)
             return emptied
 
-        def add_bias(emptied):
-            for piece, finished in enumerate(emptied):
-                nc.vector.tensor_tensor(
-                    out=finished[:].rearrange("m b t h w -> m b (t h w)"),
-                    in0=finished[:].rearrange("m b t h w -> m b (t h w)"),
-                    in1=bias_rows[:, piece * T_PER_STORE : (piece + 1) * T_PER_STORE]
-                    .rearrange("m t h w -> m (t h w)")
-                    .unsqueeze(1)
-                    .to_broadcast([P, B_HALF, T_PER_STORE * H * W]),
-                    op=mybir.AluOpType.add,
-                )
+        def add_bias(emptied, first_t):
+            n = first_t % T_PER_STORE
+            values = emptied[first_t // T_PER_STORE][:, :, n : n + T_PER_ADD].rearrange(
+                "m b t h w -> m b (t h w)"
+            )
+            nc.vector.tensor_tensor(
+                out=values,
+                in0=values,
+                in1=bias_rows[:, first_t : first_t + T_PER_ADD]
+                .rearrange("m t h w -> m (t h w)")
+                .unsqueeze(1)
+                .to_broadcast([P, B_HALF, T_PER_ADD * H * W]),
+                op=mybir.AluOpType.add,
+            )
 
         def store(half, first_t, count, finished):
             nc.sync.dma_start(
@@ -298,7 +308,7 @@ def tile_scatterhorizontal_t_kernel(
             x_raw, x_grouped = step_tiles()
             load_x(half, i, x_raw, both_passes)
             weights_load(last_load)
-            regroup(i, x_raw, x_grouped, both_passes)
+            regroup(i, x_raw, x_grouped, both_passes, scalar_share[i])
             for n in range(WARM_UP):
                 unread = psum.tile([P, SLOTS * ROWS], F32, tag="bank%d" % (n % T_PER_LOAD))
                 nc.tensor.matmul(unread[:], lhsT=zeros[:, 0:P], rhs=zeros[:], start=True, stop=True)
@@ -311,7 +321,7 @@ def tile_scatterhorizontal_t_kernel(
                 half, i = steps[k]
                 x_raw, x_grouped = step_tiles()
                 load_x(half, i, x_raw, both_passes)
-                regroup(i, x_raw, x_grouped, both_passes)
+                regroup(i, x_raw, x_grouped, both_passes, 0 if k == HANDOVER else scalar_share[i])
                 if last_load + k - 1 < len(w_pairs):
                     weights_codes(last_load + k - 1)
                 quantise_x(i, x_grouped, both_passes)
@@ -322,8 +332,10 @@ def tile_scatterhorizontal_t_kernel(
             for n, (half, i) in enumerate(steps):
                 if n + LEAD < len(steps):
                     make_ready(n + LEAD)
+                add = n + LEAD - (len(steps) - 2 - O_TILES // T_PER_ADD)
+                if 0 <= add < O_TILES // T_PER_ADD:
+                    add_bias(emptied, add * T_PER_ADD)
                 if n + LEAD == len(steps) - 1:
-                    add_bias(emptied)
                     for piece, finished in enumerate(emptied):
                         store(0, piece * T_PER_STORE, T_PER_STORE, finished)
                 if i == OFFSET_ORDER[0]:

@@ -26,9 +26,8 @@ RUN_PITCH = 256
 
 T_PER_LOAD = 4
 T_PER_QUANT = 2
-FIRST_LOAD_PIECES = 4
+LOAD_PIECES = 4
 
-WARM_UP = 8
 LEAD = 2
 
 T_PER_ADD = 2
@@ -80,25 +79,22 @@ def tile_scatterhorizontal_t_kernel(
         make_identity(nc, identity[:])
 
         bias_raw = keep.tile([P, NOFF, O_TILES], BF16)
-        nc.scalar.dma_start(out=bias_raw[:], in_=bias.rearrange("i (m t) -> m i t", t=O_TILES))
         bias_sum = keep.tile([P, O_TILES, W], F32)
-        for c in range(W):
-            first = max(0, c + PAD - (W - 1))
-            last = min(NOFF - 1, c + PAD)
-            nc.vector.tensor_reduce(
-                out=bias_sum[:, :, c],
-                in_=bias_raw[:, first : last + 1, :].rearrange("p i t -> p t i"),
-                axis=mybir.AxisListType.X,
-                op=mybir.AluOpType.add,
-            )
-
         bias_rows = keep.tile([P, O_TILES, H, W], F32)
-        nc.vector.tensor_copy(
-            out=bias_rows[:], in_=bias_sum[:].unsqueeze(2).to_broadcast([P, O_TILES, H, W])
-        )
 
-        zeros = keep.tile([P, SLOTS * ROWS], BF16)
-        nc.vector.memset(zeros[:], 0.0)
+        def add_up_bias():
+            for c in range(W):
+                first = max(0, c + PAD - (W - 1))
+                last = min(NOFF - 1, c + PAD)
+                nc.vector.tensor_reduce(
+                    out=bias_sum[:, :, c],
+                    in_=bias_raw[:, first : last + 1, :].rearrange("p i t -> p t i"),
+                    axis=mybir.AxisListType.X,
+                    op=mybir.AluOpType.add,
+                )
+            nc.vector.tensor_copy(
+                out=bias_rows[:], in_=bias_sum[:].unsqueeze(2).to_broadcast([P, O_TILES, H, W])
+            )
 
         w_codes = [
             keep.tile([P, O_TILES, PASSES, P], U32, name="w_codes%d" % i, align_bytes=64)
@@ -288,7 +284,7 @@ def tile_scatterhorizontal_t_kernel(
 
             def weights_load(n):
                 w_raws[n // pairs_per_load] = load_weights(
-                    w_pairs[n][0], w_pairs[n][1] // T_PER_LOAD, FIRST_LOAD_PIECES if n == 0 else 1
+                    w_pairs[n][0], w_pairs[n][1] // T_PER_LOAD, LOAD_PIECES if n in (0, last_load) else 1
                 )
 
             def weights_pair(n):
@@ -306,21 +302,26 @@ def tile_scatterhorizontal_t_kernel(
 
             half, i = steps[0]
             x_raw, x_grouped = step_tiles()
-            load_x(half, i, x_raw, both_passes)
+            x_raw_late = raw_pool.tile([P, B_HALF, PASSES, RUN_PITCH], BF16, tag="raw", align_bytes=256)
+            load_x(half, i, x_raw, both_passes[:1])
             weights_load(last_load)
-            regroup(i, x_raw, x_grouped, both_passes, scalar_share[i])
-            for n in range(WARM_UP):
-                unread = psum.tile([P, SLOTS * ROWS], F32, tag="bank%d" % (n % T_PER_LOAD))
-                nc.tensor.matmul(unread[:], lhsT=zeros[:, 0:P], rhs=zeros[:], start=True, stop=True)
+            load_x(half, i, x_raw_late, both_passes[1:])
+            regroup(i, x_raw, x_grouped, both_passes[:1], scalar_share[i])
             weights_pair(last_load)
             weights_codes(last_load - 1)
-            quantise_x(i, x_grouped, both_passes)
+            quantise_x(i, x_grouped, both_passes[:1])
             weights_pair(last_load + 1)
+            regroup(i, x_raw_late, x_grouped, both_passes[1:], scalar_share[i])
+            quantise_x(i, x_grouped, both_passes[1:])
 
             def make_ready(k):
                 half, i = steps[k]
                 x_raw, x_grouped = step_tiles()
                 load_x(half, i, x_raw, both_passes)
+                if k == NOFF:
+                    nc.sync.dma_start(
+                        out=bias_raw[:], in_=bias.rearrange("i (m t) -> m i t", t=O_TILES)
+                    )
                 regroup(i, x_raw, x_grouped, both_passes, 0 if k == HANDOVER else scalar_share[i])
                 if last_load + k - 1 < len(w_pairs):
                     weights_codes(last_load + k - 1)
@@ -332,6 +333,8 @@ def tile_scatterhorizontal_t_kernel(
             for n, (half, i) in enumerate(steps):
                 if n + LEAD < len(steps):
                     make_ready(n + LEAD)
+                if n + LEAD == HANDOVER:
+                    add_up_bias()
                 add = n + LEAD - (len(steps) - 2 - O_TILES // T_PER_ADD)
                 if 0 <= add < O_TILES // T_PER_ADD:
                     add_bias(emptied, add * T_PER_ADD)
@@ -343,9 +346,11 @@ def tile_scatterhorizontal_t_kernel(
                         psum.tile([P, SLOTS, ROWS], F32, tag="bank%d" % t, name="sums%d" % t)
                         for t in range(O_TILES)
                     ]
-                    for t in range(O_TILES):
-                        for g in both_passes:
-                            products(i, t, g, sums)
+                    order = [(t, g) for t in range(O_TILES) for g in both_passes]
+                    if n == 0:
+                        order = [(t, g) for g in both_passes for t in range(O_TILES)]
+                    for t, g in order:
+                        products(i, t, g, sums)
                 elif i == OFFSET_ORDER[-1]:
                     for t in range(O_TILES):
                         for late in OFFSET_ORDER[-2:]:

import concourse.mybir as mybir
from concourse.masks import make_identity

BF16 = mybir.dt.bfloat16
F32 = mybir.dt.float32
I32 = mybir.dt.int32
U32 = mybir.dt.uint32
U8 = mybir.dt.uint8
FP8X4 = mybir.dt.float8_e4m3fn_x4

B, CIN, COUT, H, W, NOFF, PAD = 16, 1024, 1024, 8, 7, 9, 4

P = 128
PACK = 4
PASSES = CIN // (P * PACK)
PAIRS = PACK // 2
O_TILES = COUT // P

HALVES = 2
B_HALF = B // HALVES
ROWS = B_HALF * H
SLOTS = 8

RUN = PACK * H * W
RUN_PITCH = 256

T_PER_LOAD = 4
T_PER_QUANT = 2
LOAD_PIECES = 4

LEAD = 2

T_PER_ADD = 2
T_PER_STORE = 4
LAST_STORES = [4, 4]

MOST_SLOTS = 4

HANDOVER = NOFF - 1 + LEAD

OFFSET_ORDER = sorted(range(NOFF), key=lambda i: abs(i - PAD))

FLOPS = 2 * COUT * CIN * B * H * sum(W - abs(i - PAD) for i in range(NOFF))


def power_of_two_pieces(count):
    pieces = []
    start = 0
    size = SLOTS
    while start < count:
        if size <= count - start:
            pieces.append((start, size))
            start += size
        else:
            size //= 2
    return pieces


def tile_scatterhorizontal_t_kernel(
    tc, x0, x1, x2, x3, x4, x5, x6, x7, x8, weights, bias, out
):
    nc = tc.nc
    xs = [x0, x1, x2, x3, x4, x5, x6, x7, x8]

    w_rows = weights.rearrange("i (m t) k -> i m (t k)", t=O_TILES)
    out_rows = out.rearrange("b (m t) h w -> m b t (h w)", t=O_TILES)

    used = [W - abs(i - PAD) for i in range(NOFF)]
    padded = [n + n % 2 for n in used]

    with (
        tc.tile_pool(name="keep", bufs=1) as keep,
        tc.tile_pool(name="raw", bufs=6) as raw_pool,
        tc.tile_pool(name="stage", bufs=4) as stage,
        tc.tile_pool(name="result", bufs=HALVES * O_TILES // T_PER_STORE) as result,
        tc.psum_pool(name="psum", bufs=1) as psum,
    ):
        identity = keep.tile([P, P], F32)
        make_identity(nc, identity[:])

        bias_raw = keep.tile([P, NOFF, O_TILES], BF16)
        bias_sum = keep.tile([P, O_TILES, W], F32)
        bias_rows = keep.tile([P, O_TILES, H, W], F32)

        def add_up_bias():
            for c in range(W):
                first = max(0, c + PAD - (W - 1))
                last = min(NOFF - 1, c + PAD)
                nc.vector.tensor_reduce(
                    out=bias_sum[:, :, c],
                    in_=bias_raw[:, first : last + 1, :].rearrange("p i t -> p t i"),
                    axis=mybir.AxisListType.X,
                    op=mybir.AluOpType.add,
                )
            nc.vector.tensor_copy(
                out=bias_rows[:], in_=bias_sum[:].unsqueeze(2).to_broadcast([P, O_TILES, H, W])
            )

        w_codes = [
            keep.tile([P, O_TILES, PASSES, P], U32, name="w_codes%d" % i, align_bytes=64)
            for i in range(NOFF)
        ]
        w_scales = [
            keep.tile([P, O_TILES, PASSES, P], U8, name="w_scales%d" % i, align_bytes=64)
            for i in range(NOFF)
        ]
        x_codes = [
            keep.tile([P, PASSES, padded[i], ROWS], U32, name="x_codes%d" % i, align_bytes=64)
            for i in range(NOFF)
        ]
        x_scales = [
            keep.tile([P, PASSES, padded[i], ROWS], U8, name="x_scales%d" % i, align_bytes=64)
            for i in range(NOFF)
        ]
        for i in range(NOFF):
            if padded[i] > used[i]:
                nc.vector.memset(x_codes[i][:, :, used[i], :].bitcast(I32), 0)
                nc.vector.memset(x_scales[i][:, :, used[i], :].bitcast(I32), 0)

        def load_weights(i, load, pieces):
            w_raw = raw_pool.tile([P, T_PER_LOAD * CIN], BF16, tag="raw", align_bytes=256)
            width = T_PER_LOAD * CIN // pieces
            for piece in range(pieces):
                nc.sync.dma_start(
                    out=w_raw[:, piece * width : (piece + 1) * width],
                    in_=w_rows[
                        i,
                        :,
                        load * T_PER_LOAD * CIN + piece * width : load * T_PER_LOAD * CIN
                        + (piece + 1) * width,
                    ],
                )
            return w_raw

        def flip_weights(w_raw, first_t):
            w_words = w_raw[:].bitcast(F32).rearrange(
                "m (t g q u) -> m t g u q", t=T_PER_LOAD, g=PASSES, u=PAIRS
            )
            w_grouped = stage.tile([P, T_PER_QUANT * CIN], BF16, tag="grouped", align_bytes=64)
            w_grouped_words = w_grouped[:].bitcast(F32).rearrange(
                "q (t g m u) -> q t g m u", t=T_PER_QUANT, g=PASSES, u=PAIRS
            )
            for n in range(T_PER_QUANT):
                t = first_t + n
                flipped = psum.tile([P, PASSES, PAIRS, P], F32, tag="bank%d" % t)
                for g in range(PASSES):
                    for u in range(PAIRS):
                        nc.tensor.transpose(
                            flipped[:, g, u, :], w_words[:, t % T_PER_LOAD, g, u, :], identity[:]
                        )
                copy = nc.vector.tensor_copy if t % 4 == 3 else nc.scalar.copy
                copy(out=w_grouped_words[:, n], in_=flipped[:].rearrange("q g u m -> q g m u"))
            return w_grouped

        def quantise_weights(i, first_t, w_grouped):
            nc.vector.quantize_mx(
                out=w_codes[i][:, first_t : first_t + T_PER_QUANT]
                .rearrange("q t g m -> q (t g m)")
                .bitcast(FP8X4),
                scales=w_scales[i][:, first_t : first_t + T_PER_QUANT].rearrange(
                    "q t g m -> q (t g m)"
                ),
                in_=w_grouped[:],
            )

        steps = [(half, i) for half in range(HALVES) for i in OFFSET_ORDER]
        both_passes = list(range(PASSES))
        scalar_share = [n // 2 if n > 3 else 0 for n in used]

        def step_tiles():
            x_raw = raw_pool.tile([P, B_HALF, PASSES, RUN_PITCH], BF16, tag="raw", align_bytes=256)
            x_grouped = stage.tile([P, PASSES, W, ROWS * PACK], BF16, tag="grouped", align_bytes=64)
            return x_raw, x_grouped

        def load_x(half, i, x_raw, passes):
            some = slice(passes[0], passes[-1] + 1)
            nc.sync.dma_start(
                out=x_raw[:, :, some, 0:RUN],
                in_=xs[i].rearrange("b (g p j) h w -> p b g (j h w)", g=PASSES, p=P, j=PACK)[:, half * B_HALF : (half + 1) * B_HALF, some],
            )

        def regroup(i, x_raw, x_grouped, passes, scalar_slots):
            first_source = max(0, PAD - i)
            x_columns = x_raw[:, :, :, 0:RUN].rearrange(
                "p b g (j h w) -> p g b h j w", j=PACK, h=H, w=W
            )
            x_grouped_values = x_grouped[:].rearrange(
                "p g s (b h j) -> p g b h j s", b=B_HALF, h=H, j=PACK
            )
            vector_slots = used[i] - scalar_slots
            for g in passes:
                for s in range(0, vector_slots, MOST_SLOTS):
                    end = min(s + MOST_SLOTS, vector_slots)
                    nc.vector.tensor_copy(
                        out=x_grouped_values[:, g, :, :, :, s:end],
                        in_=x_columns[:, g, :, :, :, first_source + s : first_source + end],
                    )
                if scalar_slots > 0:
                    nc.scalar.copy(
                        out=x_grouped_values[:, g, :, :, :, vector_slots : used[i]],
                        in_=x_columns[:, g, :, :, :, first_source + vector_slots : first_source + used[i]],
                    )

        def quantise_x(i, x_grouped, passes):
            for g in passes:
                for s, n in power_of_two_pieces(used[i]):
                    nc.vector.quantize_mx(
                        out=x_codes[i][:, g, s : s + n].rearrange("p s r -> p (s r)").bitcast(FP8X4),
                        scales=x_scales[i][:, g, s : s + n].rearrange("p s r -> p (s r)"),
                        in_=x_grouped[:, g, s : s + n].rearrange("p s v -> p (s v)"),
                    )

        def products(i, t, g, sums):
            first_slot = max(0, i - PAD)
            for s, n in power_of_two_pieces(padded[i]):
                nc.tensor.matmul_mx(
                    out=sums[t][:, first_slot + s : first_slot + s + n].rearrange("m s r -> m (s r)"),
                    lhsT=w_codes[i][:, t, g, :].bitcast(FP8X4),
                    lhsT_scale=w_scales[i][:, t, g, :],
                    rhs=x_codes[i][:, g, s : s + n].rearrange("p s r -> p (s r)").bitcast(FP8X4),
                    rhs_scale=x_scales[i][:, g, s : s + n].rearrange("p s r -> p (s r)"),
                    start=(i == OFFSET_ORDER[0] and g == 0),
                    stop=(i == OFFSET_ORDER[-1] and g == PASSES - 1 and s + n == padded[i]),
                )

        def evacuate(sums):
            emptied = []
            for first_t in range(0, O_TILES, T_PER_STORE):
                finished = result.tile([P, B_HALF, T_PER_STORE, H, W], F32)
                for n in range(T_PER_STORE):
                    nc.scalar.copy(
                        out=finished[:, :, n],
                        in_=sums[first_t + n][:, 0:W, :].rearrange("m c (b h) -> m b h c", b=B_HALF),
                    )
                emptied.append(finished)
            return emptied

        def add_bias(emptied, first_t):
            n = first_t % T_PER_STORE
            values = emptied[first_t // T_PER_STORE][:, :, n : n + T_PER_ADD].rearrange(
                "m b t h w -> m b (t h w)"
            )
            nc.vector.tensor_tensor(
                out=values,
                in0=values,
                in1=bias_rows[:, first_t : first_t + T_PER_ADD]
                .rearrange("m t h w -> m (t h w)")
                .unsqueeze(1)
                .to_broadcast([P, B_HALF, T_PER_ADD * H * W]),
                op=mybir.AluOpType.add,
            )

        def store(half, first_t, count, finished):
            nc.sync.dma_start(
                out=out_rows[:, half * B_HALF : (half + 1) * B_HALF, first_t : first_t + count],
                in_=finished[:, :, 0:count].rearrange("m b t h w -> m b t (h w)"),
            )

        def finish(half, sums):
            first_t = 0
            for count in LAST_STORES:
                finished = result.tile([P, B_HALF, T_PER_STORE, H, W], F32)
                for n in range(count):
                    nc.vector.tensor_tensor(
                        out=finished[:, :, n],
                        in0=sums[first_t + n][:, 0:W, :].rearrange("m c (b h) -> m b h c", b=B_HALF),
                        in1=bias_sum[:, first_t + n, :]
                        .unsqueeze(1)
                        .unsqueeze(1)
                        .to_broadcast([P, B_HALF, H, W]),
                        op=mybir.AluOpType.add,
                    )
                store(half, first_t, count, finished)
                first_t += count

        with tc.manual_schedule():
            w_pairs = [
                (i, first_t) for i in OFFSET_ORDER for first_t in range(0, O_TILES, T_PER_QUANT)
            ]
            pairs_per_load = T_PER_LOAD // T_PER_QUANT
            last_load = len(w_pairs) - pairs_per_load
            w_raws = {}
            copied = {}

            def weights_load(n):
                w_raws[n // pairs_per_load] = load_weights(
                    w_pairs[n][0], w_pairs[n][1] // T_PER_LOAD, LOAD_PIECES if n in (0, last_load) else 1
                )

            def weights_pair(n):
                copied[n] = flip_weights(w_raws[n // pairs_per_load], w_pairs[n][1])

            def weights_codes(n):
                quantise_weights(w_pairs[n][0], w_pairs[n][1], copied[n])

            for n in range(last_load):
                if n % pairs_per_load == 0:
                    weights_load(n)
                weights_pair(n)
                if n > 0:
                    weights_codes(n - 1)

            half, i = steps[0]
            x_raw, x_grouped = step_tiles()
            x_raw_late = raw_pool.tile([P, B_HALF, PASSES, RUN_PITCH], BF16, tag="raw", align_bytes=256)
            load_x(half, i, x_raw, both_passes[:1])
            weights_load(last_load)
            load_x(half, i, x_raw_late, both_passes[1:])
            regroup(i, x_raw, x_grouped, both_passes[:1], scalar_share[i])
            weights_pair(last_load)
            weights_codes(last_load - 1)
            quantise_x(i, x_grouped, both_passes[:1])
            weights_pair(last_load + 1)
            regroup(i, x_raw_late, x_grouped, both_passes[1:], scalar_share[i])
            quantise_x(i, x_grouped, both_passes[1:])

            def make_ready(k):
                half, i = steps[k]
                x_raw, x_grouped = step_tiles()
                load_x(half, i, x_raw, both_passes)
                if k == NOFF:
                    nc.sync.dma_start(
                        out=bias_raw[:], in_=bias.rearrange("i (m t) -> m i t", t=O_TILES)
                    )
                regroup(i, x_raw, x_grouped, both_passes, 0 if k == HANDOVER else scalar_share[i])
                if last_load + k - 1 < len(w_pairs):
                    weights_codes(last_load + k - 1)
                quantise_x(i, x_grouped, both_passes)

            for k in range(1, LEAD):
                make_ready(k)

            for n, (half, i) in enumerate(steps):
                if n + LEAD < len(steps):
                    make_ready(n + LEAD)
                if n + LEAD == HANDOVER:
                    add_up_bias()
                add = n + LEAD - (len(steps) - 2 - O_TILES // T_PER_ADD)
                if 0 <= add < O_TILES // T_PER_ADD:
                    add_bias(emptied, add * T_PER_ADD)
                if n + LEAD == len(steps) - 1:
                    for piece, finished in enumerate(emptied):
                        store(0, piece * T_PER_STORE, T_PER_STORE, finished)
                if i == OFFSET_ORDER[0]:
                    sums = [
                        psum.tile([P, SLOTS, ROWS], F32, tag="bank%d" % t, name="sums%d" % t)
                        for t in range(O_TILES)
                    ]
                    order = [(t, g) for t in range(O_TILES) for g in both_passes]
                    if n == 0:
                        order = [(t, g) for g in both_passes for t in range(O_TILES)]
                    for t, g in order:
                        products(i, t, g, sums)
                elif i == OFFSET_ORDER[-1]:
                    for t in range(O_TILES):
                        for late in OFFSET_ORDER[-2:]:
                            for g in both_passes:
                                products(late, t, g, sums)
                    if half < HALVES - 1:
                        emptied = evacuate(sums)
                elif i != OFFSET_ORDER[-2]:
                    for t in range(O_TILES):
                        for g in both_passes:
                            products(i, t, g, sums)
            finish(HALVES - 1, sums)
